import numpy as np
import ml_dtypes


def mxq(x, axis, fmt="e4m3"):
    dtype, down = {"e4m3": (ml_dtypes.float8_e4m3fn, 7), "e5m2": (ml_dtypes.float8_e5m2, 14)}[fmt]
    v = np.moveaxis(np.asarray(x, np.float32).astype(ml_dtypes.bfloat16).astype(np.float64), axis, -1)
    blocks = v.reshape(v.shape[:-1] + (-1, 32))
    amax = np.abs(blocks).max(-1, keepdims=True)
    byte = np.maximum(np.where(amax > 0, np.frexp(amax)[1] - 1 + 127, 0) - down, 1)
    scale = np.exp2(byte - 127.0)
    codes = (blocks / scale).astype(np.float32).astype(dtype).astype(np.float64)
    return np.moveaxis((codes * scale).reshape(v.shape), -1, axis)


WIDE = False


def mx_kscale(k):
    if not WIDE:
        return np.ones(k)
    levels = np.array([10, -10, 5, -5, 0])
    if k % 512:
        return np.exp2(np.random.permutation(np.resize(levels, k // 32))).repeat(32)
    a = np.empty((k // 512, 16))
    for p in range(k // 512):
        a[p, :8] = np.random.permutation(np.resize(levels, 8))
        for g in range(8):
            far = levels[np.abs(levels - a[p, g]) >= 10]
            a[p, g + 8] = far[np.random.randint(len(far))]
    return np.exp2(a.ravel()).repeat(32)


BF16 = ml_dtypes.bfloat16


def bf(x):
    return np.asarray(x, np.float32).astype(BF16)


def f64(x):
    return np.asarray(x).astype(np.float64)


B, S, HID, H, DH = 1, 512, 2048, 16, 128
INNER = H * DH
HALF = DH // 2
ROPE_BASE = 10000.0


def heads(y):
    return y.reshape(B, S, H, DH).transpose(0, 2, 1, 3)


def apply_rope(x):
    inv_freq = 1.0 / ROPE_BASE ** (np.arange(0, DH, 2) / DH)
    freqs = np.arange(S)[:, None] * inv_freq[None, :]
    cos = np.concatenate([np.cos(freqs)] * 2, -1)
    sin = np.concatenate([np.sin(freqs)] * 2, -1)
    x1, x2 = x[..., :HALF], x[..., HALF:]
    rotated = np.concatenate([-x2, x1], -1)
    return x * cos[None, None] + rotated * sin[None, None]


def draw0():
    s = mx_kscale(HID)
    return {"hidden_states": bf(np.random.standard_normal((B, S, HID)) * s),
            "Wq": bf(np.random.standard_normal((INNER, HID)) * 1.2 / np.sqrt(HID) / s),
            "bq": bf(np.random.standard_normal(INNER) * 0.3),
            "Wk": bf(np.random.standard_normal((INNER, HID)) * 1.2 / np.sqrt(HID) / s),
            "bk": bf(np.random.standard_normal(INNER) * 0.3)}


def core(hidden_states, Wq, bq, Wk, bk):
    xq = mxq(f64(hidden_states), 2, "e4m3")
    q = heads((xq @ mxq(f64(Wq).T, 0, "e4m3")) + f64(bq))
    k = heads((xq @ mxq(f64(Wk).T, 0, "e4m3")) + f64(bk))
    return apply_rope(q), apply_rope(k)


def e4m3fn_bytes(y):
    return np.clip(np.asarray(y, np.float64), -448.0, 448.0).astype(np.float32).astype(ml_dtypes.float8_e4m3fn).view(np.uint8)


def e4m3fn_values(b):
    return np.asarray(b, np.uint8).view(ml_dtypes.float8_e4m3fn).astype(np.float64)


def setup_inputs():
    d = draw0()
    x0 = np.asarray(d['Wq']).astype(np.float64)
    s = (np.max(np.abs(x0), axis=(0,), keepdims=True) / 448.0).astype(np.float32)
    out = {}
    for k, v in d.items():
        if k == 'Wq':
            out['Wq_bytes'] = e4m3fn_bytes(x0 / s.astype(np.float64))
            out['Wq_scale'] = s
        else:
            out[k] = v
    return out


def reference(hidden_states, Wq_bytes, Wq_scale, bq, Wk, bk):
    return core(hidden_states, e4m3fn_values(Wq_bytes) * Wq_scale.astype(np.float64), bq, Wk, bk)

@@ -1,0 +1,270 @@
+import math
+from contextlib import ExitStack
+
+import concourse.mybir as mybir
+from concourse.masks import make_identity
+
+F32 = mybir.dt.float32
+BF16 = mybir.dt.bfloat16
+U32 = mybir.dt.uint32
+U8 = mybir.dt.uint8
+I32 = mybir.dt.int32
+FP8 = mybir.dt.float8_e4m3fn
+FP8X4 = mybir.dt.float8_e4m3fn_x4
+ALU = mybir.AluOpType
+ACT = mybir.ActivationFunctionType
+
+P = 128
+TOK = 512
+HID = 2048
+HEADS = 16
+DH = 128
+PASSES = 4
+FLOPS = 2 * 2 * TOK * HID * HID
+
+MANUAL = True
+LAG_Q = 1
+LAG_M = 1
+LAG_Z = 2
+LAG_F = 3
+
+TWO_PI = 2.0 * math.pi
+C1 = 6.28125
+C2 = TWO_PI - C1
+
+
+def tile_densemha_pa_kernel(tc, hidden_states, Wq_bytes, Wq_scale, bq, Wk, bk, out_0, out_1):
+    nc = tc.nc
+    with ExitStack() as ctx:
+        const = ctx.enter_context(tc.tile_pool(name="const", bufs=1))
+        work = ctx.enter_context(tc.tile_pool(name="work", bufs=3))
+        psum = ctx.enter_context(tc.psum_pool(name="psum", bufs=2))
+        if MANUAL:
+            ctx.enter_context(tc.manual_schedule())
+
+        seq = [("k", 0), ("k", 1)]
+        for j in range(HEADS - 2):
+            seq.append(("q", j))
+            seq.append(("k", j + 2))
+        seq.append(("q", HEADS - 2))
+        seq.append(("q", HEADS - 1))
+        n_x = 4
+        units = [("x", a) for a in range(n_x)] + seq
+        n_units = len(units)
+
+        x_view = hidden_states[0].rearrange("(p a) k -> a p k", a=4)
+        x_sb = []
+        for a in range(n_x):
+            xt = const.tile([P, HID], BF16, name="x_sb%d" % a, tag="x_sb%d" % a)
+            nc.sync.dma_start(out=xt[:], in_=x_view[a])
+            x_sb.append(xt)
+        scale_bc = const.tile([P, HID], F32, name="scale_bc", tag="scale_bc")
+        wq_view = Wq_bytes.rearrange("(h n) k -> h n k", n=P)
+        wk_view = Wk.rearrange("(h n) k -> h n k", n=P)
+        w_in = {}
+        first_q = True
+        for kind, h in seq:
+            if kind == "q":
+                if first_q:
+                    nc.sync.dma_start(out=scale_bc[:], in_=Wq_scale.rearrange("o k -> (o k)").partition_broadcast(P))
+                    first_q = False
+                wt = const.tile([P, HID], U8, name="wq_bytes%d" % h, tag="wq_bytes%d" % h)
+                nc.sync.dma_start(out=wt[:], in_=wq_view[h])
+            else:
+                wt = const.tile([P, HID], BF16, name="wk_sb%d" % h, tag="wk_sb%d" % h)
+                nc.sync.dma_start(out=wt[:], in_=wk_view[h])
+            w_in[(kind, h)] = wt
+
+        dmy = const.tile([P, 1], F32, name="dmy", tag="dmy")
+        dmy2 = const.tile([P, 1], F32, name="dmy2", tag="dmy2")
+        nc.gpsimd.memset(dmy[:], 0.0)
+        bb = const.tile([P, P], BF16, name="bb", tag="bb")
+        nc.vector.memset(bb[:], 0.0)
+        nc.scalar.dma_start(out=bb[0:HEADS, :], in_=bq.rearrange("(h d) -> h d", d=DH))
+        nc.scalar.dma_start(out=bb[HEADS:2 * HEADS, :], in_=bk.rearrange("(h d) -> h d", d=DH))
+        nc.scalar.activation(out=dmy2[:], in_=dmy[:], func=ACT.Sin)
+
+        ident = const.tile([P, P], F32, name="ident", tag="ident")
+        make_identity(nc, ident[:])
+        tok = const.tile([P, TOK], F32, name="tok", tag="tok")
+        nc.gpsimd.iota(out=tok[:], pattern=[[1, 4], [4, P]], base=0, channel_multiplier=0,
+                       allow_small_or_imprecise_dtypes=True)
+
+        th = const.tile([P, P], F32, name="th", tag="th")
+        ratio = 10000.0 ** (-1.0 / 64.0)
+        nc.vector.memset(th[:, 0:1], 1.0)
+        for w in (1, 2, 4, 8, 16, 32):
+            nc.vector.tensor_scalar(out=th[:, w:2 * w], in0=th[:, 0:w], scalar1=ratio ** w, scalar2=None, op0=ALU.mult)
+        nc.vector.tensor_scalar(out=th[:, 64:128], in0=th[:, 0:64], scalar1=-1.0, scalar2=None, op0=ALU.mult)
+        thp = psum.tile([P, 512], F32, name="thp", tag="fin", bufs=2)
+        nc.tensor.transpose(out=thp[:, 0:P], in_=th[:], identity=ident[:])
+        thc = const.tile([P, 1], F32, name="thc", tag="thc")
+        nc.vector.tensor_copy(out=thc[:], in_=thp[:, 0:1])
+        perm = const.tile([P, P], F32, name="perm", tag="perm")
+        nc.vector.tensor_copy(out=perm[:, 0:64], in_=ident[:, 64:128])
+        nc.vector.tensor_copy(out=perm[:, 64:128], in_=ident[:, 0:64])
+
+        ang = const.tile([P, TOK], F32, name="ang", tag="ang")
+        nc.gpsimd.tensor_scalar(out=ang[:], in0=tok[:], scalar1=thc[:, 0:1], scalar2=0.0, op0=ALU.mult, op1=ALU.add)
+        yi = const.tile([P, TOK], I32, name="yi", tag="yi")
+        nc.gpsimd.tensor_scalar(out=yi[:], in0=ang[:], scalar1=1.0 / TWO_PI, scalar2=127.875, op0=ALU.mult, op1=ALU.add)
+
+        nf = const.tile([P, TOK], F32, name="nf", tag="nf")
+        r1 = const.tile([P, TOK], F32, name="r1", tag="r1")
+        r2 = const.tile([P, TOK], F32, name="r2", tag="r2")
+        t1 = const.tile([P, TOK], F32, name="t1", tag="t1")
+        rs = const.tile([P, TOK], F32, name="rs", tag="rs")
+        rc = const.tile([P, TOK], F32, name="rc", tag="rc")
+        sin_t = const.tile([P, TOK], F32, name="sin_t", tag="sin_t")
+        cos_t = const.tile([P, TOK], F32, name="cos_t", tag="cos_t")
+        bbf = const.tile([P, P], F32, name="bbf", tag="bbf")
+        bias = const.tile([P, 2 * HEADS], F32, name="bias", tag="bias")
+
+        def table_part_a():
+            nc.vector.tensor_scalar(out=nf[:], in0=yi[:], scalar1=-128.0, scalar2=None, op0=ALU.add)
+            nc.vector.scalar_tensor_tensor(out=r1[:], in0=nf[:], scalar=-C1, in1=ang[:], op0=ALU.mult, op1=ALU.add)
+            nc.vector.scalar_tensor_tensor(out=r2[:], in0=nf[:], scalar=-C2, in1=r1[:], op0=ALU.mult, op1=ALU.add)
+
+        def table_part_b():
+            nc.vector.scalar_tensor_tensor(out=rc[:], in0=r2[:], scalar=-1.0, in1=r2[:], op0=ALU.mult, op1=ALU.max)
+            nc.vector.tensor_scalar(out=t1[:], in0=r2[:], scalar1=-0.5 * math.pi, scalar2=None, op0=ALU.add)
+            nc.vector.tensor_copy(out=bbf[:], in_=bb[:])
+            nc.vector.scalar_tensor_tensor(out=rs[:], in0=t1[:], scalar=-1.0, in1=t1[:], op0=ALU.mult, op1=ALU.max)
+
+        def table_part_c():
+            nc.scalar.activation(out=cos_t[:], in_=rc[:], func=ACT.Sin, bias=0.5 * math.pi, scale=-1.0)
+            nc.scalar.activation(out=sin_t[:], in_=rs[:], func=ACT.Sin, bias=0.5 * math.pi, scale=-1.0)
+            bp = psum.tile([P, 512], F32, name="bp", tag="acc", bufs=2)
+            nc.tensor.transpose(out=bp[:, 0:P], in_=bbf[:], identity=ident[:])
+            nc.vector.tensor_copy(out=bias[:], in_=bp[:, 0:2 * HEADS])
+
+        xc = []
+        xs = []
+        for g in range(PASSES):
+            xc.append(const.tile([P, TOK], U32, name="xc%d" % g, tag="xc%d" % g, align_bytes=64))
+            xs.append(const.tile([P, TOK], U8, name="xs%d" % g, tag="xs%d" % g, align_bytes=64))
+
+        st = {}
+
+        def widen(j, half):
+            if half == 0:
+                st[("wbf", j)] = work.tile([P, HID], BF16, name="wbf", tag="wbf", bufs=3)
+            cols = slice(half * 1024, (half + 1) * 1024)
+            nc.vector.tensor_tensor(out=st[("wbf", j)][:, cols], in0=w_in[("q", j)][:, cols].bitcast(FP8),
+                                    in1=scale_bc[:, cols], op=ALU.mult)
+
+        def stage_t(u):
+            kind, h = units[u]
+            if kind == "x":
+                src = x_sb[h]
+            elif kind == "k":
+                src = w_in[("k", h)]
+            else:
+                src = st[("wbf", h)]
+            words = src[:].bitcast(F32)
+            banks = []
+            for j in range(2):
+                bank = psum.tile([P, 512], F32, name="tp", tag="tp", bufs=4)
+                for gl in range(2):
+                    g = 2 * j + gl
+                    for e in range(2):
+                        c0 = (2 * gl + e) * P
+                        nc.tensor.transpose(out=bank[:, c0:c0 + P], in_=words[:, 256 * g + e:256 * (g + 1):2],
+                                            identity=ident[:])
+                banks.append(bank)
+            st[("tp", u)] = banks
+
+        def stage_e(u):
+            wg = work.tile([P, HID], BF16, name="wg", tag="wg", bufs=3, align_bytes=64)
+            wgw = wg[:].bitcast(F32)
+            for j in range(2):
+                nc.scalar.copy(out=wgw[:, 512 * j:512 * (j + 1)].rearrange("p (g r e) -> p g r e", g=2, e=2),
+                               in_=st[("tp", u)][j][:].rearrange("p (g e r) -> p g r e", g=2, e=2))
+            st[("wg", u)] = wg
+
+        def stage_q(u):
+            kind, h = units[u]
+            wg = st[("wg", u)]
+            if kind == "x":
+                for g in range(PASSES):
+                    nc.vector.quantize_mx(out=xc[g][:, h * P:(h + 1) * P].bitcast(FP8X4),
+                                          scales=xs[g][:, h * P:(h + 1) * P],
+                                          in_=wg[:, g * 512:(g + 1) * 512])
+            else:
+                wc = work.tile([P, 512], U32, name="wc", tag="wc", bufs=3, align_bytes=64)
+                ws = work.tile([P, 512], U8, name="ws", tag="ws", bufs=3, align_bytes=64)
+                nc.vector.quantize_mx(out=wc[:].bitcast(FP8X4), scales=ws[:], in_=wg[:])
+                st[("wc", u)] = (wc, ws)
+
+        def stage_m(u):
+            wc, ws = st[("wc", u)]
+            acc = psum.tile([P, 512], F32, name="acc", tag="acc", bufs=2)
+            for g in range(PASSES):
+                nc.tensor.matmul_mx(out=acc[:], lhsT=wc[:, g * P:(g + 1) * P].bitcast(FP8X4),
+                                    lhsT_scale=ws[:, g * P:(g + 1) * P],
+                                    rhs=xc[g][:].bitcast(FP8X4), rhs_scale=xs[g][:],
+                                    start=(g == 0), stop=(g == PASSES - 1))
+            st[("acc", u)] = acc
+
+        def stage_z(u):
+            kind, h = units[u]
+            col = h if kind == "q" else HEADS + h
+            acc = st[("acc", u)]
+            z1 = work.tile([P, TOK], F32, name="z1", tag="z1", bufs=3)
+            z2 = work.tile([P, TOK], F32, name="z2", tag="z2", bufs=3)
+            nc.vector.scalar_tensor_tensor(out=z1[:], in0=acc[:], scalar=bias[:, col:col + 1], in1=cos_t[:],
+                                           op0=ALU.add, op1=ALU.mult)
+            nc.vector.scalar_tensor_tensor(out=z2[:], in0=acc[:], scalar=bias[:, col:col + 1], in1=sin_t[:],
+                                           op0=ALU.add, op1=ALU.mult)
+            st[("z", u)] = (z1, z2)
+
+        def stage_f(u):
+            z1, z2 = st[("z", u)]
+            fin = psum.tile([P, 512], F32, name="fin", tag="fin", bufs=2)
+            for a in range(4):
+                cols = slice(a * P, (a + 1) * P)
+                nc.tensor.matmul(out=fin[:, cols], lhsT=z1[:, cols], rhs=ident[:], is_transpose=True,
+                                 start=True, stop=False)
+                nc.tensor.matmul(out=fin[:, cols], lhsT=z2[:, cols], rhs=perm[:], is_transpose=True,
+                                 start=False, stop=True)
+            st[("fin", u)] = fin
+
+        def stage_o(u):
+            kind, h = units[u]
+            dst = out_0 if kind == "q" else out_1
+            ob = work.tile([P, TOK], F32, name="ob", tag="ob", bufs=4)
+            nc.scalar.copy(out=ob[:], in_=st[("fin", u)][:])
+            nc.scalar.dma_start(out=dst[0, h].rearrange("(p a) d -> p (a d)", a=4), in_=ob[:])
+
+        widen_at = {}
+        for u in range(n_units):
+            kind, h = units[u]
+            if kind == "q":
+                lead = 3 if h < HEADS - 1 else 2
+                widen_at[u - lead] = (h, 0)
+                widen_at[u - lead + 1] = (h, 1)
+
+        def is_head(u):
+            return n_x <= u < n_units
+
+        for u in range(n_units + LAG_F):
+            if u < n_units:
+                stage_t(u)
+                stage_e(u)
+            if 0 <= u - LAG_Q < n_units:
+                stage_q(u - LAG_Q)
+            if is_head(u - LAG_F):
+                stage_f(u - LAG_F)
+                stage_o(u - LAG_F)
+            if is_head(u - LAG_M):
+                stage_m(u - LAG_M)
+            if is_head(u - LAG_Z):
+                stage_z(u - LAG_Z)
+            if u in widen_at:
+                widen(widen_at[u][0], widen_at[u][1])
+            if u == 0:
+                table_part_a()
+            if u == 1:
+                table_part_b()
+            if u == 2:
+                table_part_c()

@@ -29,8 +29,6 @@ LAG_Z = 2
 LAG_F = 3
 
 TWO_PI = 2.0 * math.pi
-C1 = 6.28125
-C2 = TWO_PI - C1
 
 
 def tile_densemha_pa_kernel(tc, hidden_states, Wq_bytes, Wq_scale, bq, Wk, bk, out_0, out_1):
@@ -54,20 +52,21 @@ def tile_densemha_pa_kernel(tc, hidden_states, Wq_bytes, Wq_scale, bq, Wk, bk, o
 
         x_view = hidden_states[0].rearrange("(p a) k -> a p k", a=4)
         x_sb = []
-        for a in range(n_x):
-            xt = const.tile([P, HID], BF16, name="x_sb%d" % a, tag="x_sb%d" % a)
-            nc.sync.dma_start(out=xt[:], in_=x_view[a])
-            x_sb.append(xt)
+        sc_rows = const.tile([P, P], F32, name="sc_rows", tag="sc_rows")
+        nc.gpsimd.memset(sc_rows[:], 0.0)
+        nc.sync.dma_start(out=sc_rows[0:16, :], in_=Wq_scale.rearrange("o (c p) -> (o c) p", p=P))
         scale_bc = const.tile([P, HID], F32, name="scale_bc", tag="scale_bc")
         wq_view = Wq_bytes.rearrange("(h n) k -> h n k", n=P)
         wk_view = Wk.rearrange("(h n) k -> h n k", n=P)
         w_in = {}
-        first_q = True
-        for kind, h in seq:
+        load_order = [("x", 0), ("x", 1), ("x", 2), ("x", 3), ("k", 0), ("q", 0), ("k", 1)] + seq[3:]
+        for kind, h in load_order:
+            if kind == "x":
+                wt = const.tile([P, HID], BF16, name="x_sb%d" % h, tag="x_sb%d" % h)
+                nc.sync.dma_start(out=wt[:], in_=x_view[h])
+                x_sb.append(wt)
+                continue
             if kind == "q":
-                if first_q:
-                    nc.sync.dma_start(out=scale_bc[:], in_=Wq_scale.rearrange("o k -> (o k)").partition_broadcast(P))
-                    first_q = False
                 wt = const.tile([P, HID], U8, name="wq_bytes%d" % h, tag="wq_bytes%d" % h)
                 nc.sync.dma_start(out=wt[:], in_=wq_view[h])
             else:
@@ -100,19 +99,21 @@ def tile_densemha_pa_kernel(tc, hidden_states, Wq_bytes, Wq_scale, bq, Wk, bk, o
         nc.tensor.transpose(out=thp[:, 0:P], in_=th[:], identity=ident[:])
         thc = const.tile([P, 1], F32, name="thc", tag="thc")
         nc.vector.tensor_copy(out=thc[:], in_=thp[:, 0:1])
+        scp = psum.tile([P, 512], F32, name="scp", tag="acc", bufs=2)
+        nc.tensor.transpose(out=scp[:, 0:P], in_=sc_rows[:], identity=ident[:])
+        s_col = const.tile([P, 16], F32, name="s_col", tag="s_col")
+        nc.vector.tensor_copy(out=s_col[:], in_=scp[:, 0:16])
         perm = const.tile([P, P], F32, name="perm", tag="perm")
         nc.vector.tensor_copy(out=perm[:, 0:64], in_=ident[:, 64:128])
         nc.vector.tensor_copy(out=perm[:, 64:128], in_=ident[:, 0:64])
 
-        ang = const.tile([P, TOK], F32, name="ang", tag="ang")
-        nc.gpsimd.tensor_scalar(out=ang[:], in0=tok[:], scalar1=thc[:, 0:1], scalar2=0.0, op0=ALU.mult, op1=ALU.add)
-        yi = const.tile([P, TOK], I32, name="yi", tag="yi")
-        nc.gpsimd.tensor_scalar(out=yi[:], in0=ang[:], scalar1=1.0 / TWO_PI, scalar2=127.875, op0=ALU.mult, op1=ALU.add)
+        turns = const.tile([P, TOK], F32, name="turns", tag="turns")
+        nc.gpsimd.tensor_scalar(out=turns[:], in0=tok[:], scalar1=thc[:, 0:1], scalar2=1.0 / TWO_PI, op0=ALU.mult, op1=ALU.mult)
+        n_cos = const.tile([P, TOK], I32, name="n_cos", tag="n_cos")
+        nc.gpsimd.tensor_scalar(out=n_cos[:], in0=turns[:], scalar1=1.0, scalar2=0.25, op0=ALU.mult, op1=ALU.add)
+        n_sin = const.tile([P, TOK], I32, name="n_sin", tag="n_sin")
+        nc.gpsimd.tensor_scalar(out=n_sin[:], in0=turns[:], scalar1=1.0, scalar2=0.0, op0=ALU.mult, op1=ALU.add)
 
-        nf = const.tile([P, TOK], F32, name="nf", tag="nf")
-        r1 = const.tile([P, TOK], F32, name="r1", tag="r1")
-        r2 = const.tile([P, TOK], F32, name="r2", tag="r2")
-        t1 = const.tile([P, TOK], F32, name="t1", tag="t1")
         rs = const.tile([P, TOK], F32, name="rs", tag="rs")
         rc = const.tile([P, TOK], F32, name="rc", tag="rc")
         sin_t = const.tile([P, TOK], F32, name="sin_t", tag="sin_t")
@@ -120,20 +121,16 @@ def tile_densemha_pa_kernel(tc, hidden_states, Wq_bytes, Wq_scale, bq, Wk, bk, o
         bbf = const.tile([P, P], F32, name="bbf", tag="bbf")
         bias = const.tile([P, 2 * HEADS], F32, name="bias", tag="bias")
 
-        def table_part_a():
-            nc.vector.tensor_scalar(out=nf[:], in0=yi[:], scalar1=-128.0, scalar2=None, op0=ALU.add)
-            nc.vector.scalar_tensor_tensor(out=r1[:], in0=nf[:], scalar=-C1, in1=ang[:], op0=ALU.mult, op1=ALU.add)
-            nc.vector.scalar_tensor_tensor(out=r2[:], in0=nf[:], scalar=-C2, in1=r1[:], op0=ALU.mult, op1=ALU.add)
+        def table_cos():
+            nc.vector.scalar_tensor_tensor(out=rc[:], in0=n_cos[:], scalar=-1.0, in1=turns[:], op0=ALU.mult, op1=ALU.add)
+            nc.scalar.activation(out=cos_t[:], in_=rc[:], func=ACT.Sin, bias=0.5 * math.pi, scale=TWO_PI)
 
-        def table_part_b():
-            nc.vector.scalar_tensor_tensor(out=rc[:], in0=r2[:], scalar=-1.0, in1=r2[:], op0=ALU.mult, op1=ALU.max)
-            nc.vector.tensor_scalar(out=t1[:], in0=r2[:], scalar1=-0.5 * math.pi, scalar2=None, op0=ALU.add)
+        def table_sin():
+            nc.vector.scalar_tensor_tensor(out=rs[:], in0=n_sin[:], scalar=-1.0, in1=turns[:], op0=ALU.mult, op1=ALU.add)
+            nc.scalar.activation(out=sin_t[:], in_=rs[:], func=ACT.Sin, scale=TWO_PI)
+
+        def bias_columns():
             nc.vector.tensor_copy(out=bbf[:], in_=bb[:])
-            nc.vector.scalar_tensor_tensor(out=rs[:], in0=t1[:], scalar=-1.0, in1=t1[:], op0=ALU.mult, op1=ALU.max)
-
-        def table_part_c():
-            nc.scalar.activation(out=cos_t[:], in_=rc[:], func=ACT.Sin, bias=0.5 * math.pi, scale=-1.0)
-            nc.scalar.activation(out=sin_t[:], in_=rs[:], func=ACT.Sin, bias=0.5 * math.pi, scale=-1.0)
             bp = psum.tile([P, 512], F32, name="bp", tag="acc", bufs=2)
             nc.tensor.transpose(out=bp[:, 0:P], in_=bbf[:], identity=ident[:])
             nc.vector.tensor_copy(out=bias[:], in_=bp[:, 0:2 * HEADS])
@@ -145,6 +142,24 @@ def tile_densemha_pa_kernel(tc, hidden_states, Wq_bytes, Wq_scale, bq, Wk, bk, o
             xs.append(const.tile([P, TOK], U8, name="xs%d" % g, tag="xs%d" % g, align_bytes=64))
 
         st = {}
+
+        spread = {}
+
+        def spread_transposes(half):
+            for i in range(2):
+                bank = psum.tile([P, 512], F32, name="tp", tag="tp", bufs=4)
+                for r in range(4):
+                    c = 8 * half + 4 * i + r
+                    nc.tensor.transpose(out=bank[:, r * P:(r + 1) * P], in_=s_col[:, c:c + 1].to_broadcast([P, P]),
+                                        identity=ident[:])
+                spread[2 * half + i] = bank
+
+        def spread_out(b, on_scalar):
+            dst = scale_bc[:, b * 512:(b + 1) * 512]
+            if on_scalar:
+                nc.scalar.copy(out=dst, in_=spread[b][:])
+            else:
+                nc.vector.tensor_copy(out=dst, in_=spread[b][:])
 
         def widen(j, half):
             if half == 0:
@@ -248,6 +263,14 @@ def tile_densemha_pa_kernel(tc, hidden_states, Wq_bytes, Wq_scale, bq, Wk, bk, o
             return n_x <= u < n_units
 
         for u in range(n_units + LAG_F):
+            if u == 0:
+                spread_transposes(0)
+                spread_out(0, True)
+                spread_out(1, False)
+            if u == 1:
+                spread_transposes(1)
+                spread_out(2, False)
+                spread_out(3, False)
             if u < n_units:
                 stage_t(u)
                 stage_e(u)
@@ -262,9 +285,8 @@ def tile_densemha_pa_kernel(tc, hidden_states, Wq_bytes, Wq_scale, bq, Wk, bk, o
                 stage_z(u - LAG_Z)
             if u in widen_at:
                 widen(widen_at[u][0], widen_at[u][1])
-            if u == 0:
-                table_part_a()
             if u == 1:
-                table_part_b()
+                table_cos()
             if u == 2:
-                table_part_c()
+                table_sin()
+                bias_columns()

@@ -22,11 +22,13 @@ DH = 128
 PASSES = 4
 FLOPS = 2 * 2 * TOK * HID * HID
 
-MANUAL = True
 LAG_Q = 1
 LAG_M = 1
 LAG_Z = 2
 LAG_F = 3
+AHEAD = 2
+W_FIRST = 5
+SPASS = 1
 
 TWO_PI = 2.0 * math.pi
 
@@ -37,18 +39,17 @@ def tile_densemha_pa_kernel(tc, hidden_states, Wq_bytes, Wq_scale, bq, Wk, bk, o
         const = ctx.enter_context(tc.tile_pool(name="const", bufs=1))
         work = ctx.enter_context(tc.tile_pool(name="work", bufs=3))
         psum = ctx.enter_context(tc.psum_pool(name="psum", bufs=2))
-        if MANUAL:
-            ctx.enter_context(tc.manual_schedule())
+        ctx.enter_context(tc.manual_schedule())
 
-        seq = [("k", 0), ("k", 1)]
-        for j in range(HEADS - 2):
+        seq = [("k", h) for h in range(AHEAD)]
+        for j in range(HEADS - AHEAD):
             seq.append(("q", j))
-            seq.append(("k", j + 2))
-        seq.append(("q", HEADS - 2))
-        seq.append(("q", HEADS - 1))
+            seq.append(("k", j + AHEAD))
+        seq += [("q", h) for h in range(HEADS - AHEAD, HEADS)]
         n_x = 4
         units = [("x", a) for a in range(n_x)] + seq
         n_units = len(units)
+        v_cols = HID - 512 * SPASS
 
         x_view = hidden_states[0].rearrange("(p a) k -> a p k", a=4)
         x_sb = []
@@ -59,28 +60,30 @@ def tile_densemha_pa_kernel(tc, hidden_states, Wq_bytes, Wq_scale, bq, Wk, bk, o
         wq_view = Wq_bytes.rearrange("(h n) k -> h n k", n=P)
         wk_view = Wk.rearrange("(h n) k -> h n k", n=P)
         w_in = {}
-        load_order = [("x", 0), ("x", 1), ("x", 2), ("x", 3), ("k", 0), ("q", 0), ("k", 1)] + seq[3:]
-        for kind, h in load_order:
+        for kind, h in units:
             if kind == "x":
                 wt = const.tile([P, HID], BF16, name="x_sb%d" % h, tag="x_sb%d" % h)
                 nc.sync.dma_start(out=wt[:], in_=x_view[h])
                 x_sb.append(wt)
-                continue
-            if kind == "q":
+            elif kind == "q":
                 wt = const.tile([P, HID], U8, name="wq_bytes%d" % h, tag="wq_bytes%d" % h)
                 nc.sync.dma_start(out=wt[:], in_=wq_view[h])
+                w_in[(kind, h)] = wt
             else:
                 wt = const.tile([P, HID], BF16, name="wk_sb%d" % h, tag="wk_sb%d" % h)
                 nc.sync.dma_start(out=wt[:], in_=wk_view[h])
-            w_in[(kind, h)] = wt
+                w_in[(kind, h)] = wt
 
         dmy = const.tile([P, 1], F32, name="dmy", tag="dmy")
         dmy2 = const.tile([P, 1], F32, name="dmy2", tag="dmy2")
         nc.gpsimd.memset(dmy[:], 0.0)
         bb = const.tile([P, P], BF16, name="bb", tag="bb")
         nc.vector.memset(bb[:], 0.0)
+        s_t = const.tile([P, 16], F32, name="s_t", tag="s_t")
         nc.scalar.dma_start(out=bb[0:HEADS, :], in_=bq.rearrange("(h d) -> h d", d=DH))
         nc.scalar.dma_start(out=bb[HEADS:2 * HEADS, :], in_=bk.rearrange("(h d) -> h d", d=DH))
+        nc.scalar.dma_start(out=s_t[:].rearrange("p (g t) -> p g t", t=4),
+                            in_=Wq_scale.rearrange("o (g p t) -> p (o g) t", p=P, t=4))
         nc.scalar.activation(out=dmy2[:], in_=dmy[:], func=ACT.Sin)
 
         ident = const.tile([P, P], F32, name="ident", tag="ident")
@@ -104,36 +107,25 @@ def tile_densemha_pa_kernel(tc, hidden_states, Wq_bytes, Wq_scale, bq, Wk, bk, o
         s_col = const.tile([P, 16], F32, name="s_col", tag="s_col")
         nc.vector.tensor_copy(out=s_col[:], in_=scp[:, 0:16])
         perm = const.tile([P, P], F32, name="perm", tag="perm")
-        nc.vector.tensor_copy(out=perm[:, 0:64], in_=ident[:, 64:128])
-        nc.vector.tensor_copy(out=perm[:, 64:128], in_=ident[:, 0:64])
+        bbf = const.tile([P, P], F32, name="bbf", tag="bbf")
+        bias = const.tile([P, 2 * HEADS], F32, name="bias", tag="bias")
 
         turns = const.tile([P, TOK], F32, name="turns", tag="turns")
-        nc.gpsimd.tensor_scalar(out=turns[:], in0=tok[:], scalar1=thc[:, 0:1], scalar2=1.0 / TWO_PI, op0=ALU.mult, op1=ALU.mult)
         n_cos = const.tile([P, TOK], I32, name="n_cos", tag="n_cos")
-        nc.gpsimd.tensor_scalar(out=n_cos[:], in0=turns[:], scalar1=1.0, scalar2=0.25, op0=ALU.mult, op1=ALU.add)
         n_sin = const.tile([P, TOK], I32, name="n_sin", tag="n_sin")
-        nc.gpsimd.tensor_scalar(out=n_sin[:], in0=turns[:], scalar1=1.0, scalar2=0.0, op0=ALU.mult, op1=ALU.add)
-
         rs = const.tile([P, TOK], F32, name="rs", tag="rs")
         rc = const.tile([P, TOK], F32, name="rc", tag="rc")
         sin_t = const.tile([P, TOK], F32, name="sin_t", tag="sin_t")
         cos_t = const.tile([P, TOK], F32, name="cos_t", tag="cos_t")
-        bbf = const.tile([P, P], F32, name="bbf", tag="bbf")
-        bias = const.tile([P, 2 * HEADS], F32, name="bias", tag="bias")
-
-        def table_cos():
-            nc.vector.scalar_tensor_tensor(out=rc[:], in0=n_cos[:], scalar=-1.0, in1=turns[:], op0=ALU.mult, op1=ALU.add)
-            nc.scalar.activation(out=cos_t[:], in_=rc[:], func=ACT.Sin, bias=0.5 * math.pi, scale=TWO_PI)
-
-        def table_sin():
-            nc.vector.scalar_tensor_tensor(out=rs[:], in0=n_sin[:], scalar=-1.0, in1=turns[:], op0=ALU.mult, op1=ALU.add)
-            nc.scalar.activation(out=sin_t[:], in_=rs[:], func=ACT.Sin, scale=TWO_PI)
-
-        def bias_columns():
-            nc.vector.tensor_copy(out=bbf[:], in_=bb[:])
-            bp = psum.tile([P, 512], F32, name="bp", tag="acc", bufs=2)
-            nc.tensor.transpose(out=bp[:, 0:P], in_=bbf[:], identity=ident[:])
-            nc.vector.tensor_copy(out=bias[:], in_=bp[:, 0:2 * HEADS])
+        nc.vector.tensor_scalar(out=turns[:], in0=tok[:], scalar1=thc[:, 0:1], scalar2=1.0 / TWO_PI,
+                                op0=ALU.mult, op1=ALU.mult)
+        nc.vector.tensor_copy(out=bbf[:], in_=bb[:])
+        nc.vector.tensor_scalar(out=n_cos[:], in0=turns[:], scalar1=0.25, scalar2=None, op0=ALU.add)
+        nc.vector.tensor_scalar(out=n_sin[:], in0=turns[:], scalar1=0.0, scalar2=None, op0=ALU.add)
+        nc.vector.scalar_tensor_tensor(out=rc[:], in0=n_cos[:], scalar=-1.0, in1=turns[:], op0=ALU.mult, op1=ALU.add)
+        nc.vector.scalar_tensor_tensor(out=rs[:], in0=n_sin[:], scalar=-1.0, in1=turns[:], op0=ALU.mult, op1=ALU.add)
+        nc.vector.tensor_copy(out=perm[:, 0:64], in_=ident[:, 64:128])
+        nc.vector.tensor_copy(out=perm[:, 64:128], in_=ident[:, 0:64])
 
         xc = []
         xs = []
@@ -142,8 +134,16 @@ def tile_densemha_pa_kernel(tc, hidden_states, Wq_bytes, Wq_scale, bq, Wk, bk, o
             xs.append(const.tile([P, TOK], U8, name="xs%d" % g, tag="xs%d" % g, align_bytes=64))
 
         st = {}
-
         spread = {}
+
+        def bias_columns():
+            bp = psum.tile([P, 512], F32, name="bp", tag="acc", bufs=2)
+            nc.tensor.transpose(out=bp[:, 0:P], in_=bbf[:], identity=ident[:])
+            nc.vector.tensor_copy(out=bias[:], in_=bp[:, 0:2 * HEADS])
+
+        def tables():
+            nc.scalar.activation(out=cos_t[:], in_=rc[:], func=ACT.Sin, bias=0.5 * math.pi, scale=TWO_PI)
+            nc.scalar.activation(out=sin_t[:], in_=rs[:], func=ACT.Sin, scale=TWO_PI)
 
         def spread_transposes(half):
             for i in range(2):
@@ -163,10 +163,14 @@ def tile_densemha_pa_kernel(tc, hidden_states, Wq_bytes, Wq_scale, bq, Wk, bk, o
 
         def widen(j, half):
             if half == 0:
-                st[("wbf", j)] = work.tile([P, HID], BF16, name="wbf", tag="wbf", bufs=3)
-            cols = slice(half * 1024, (half + 1) * 1024)
+                st[("wbf", j)] = work.tile([P, HID], BF16, name="wbf", tag="wbf", bufs=4)
+            cols = slice(half * v_cols // 2, (half + 1) * v_cols // 2)
             nc.vector.tensor_tensor(out=st[("wbf", j)][:, cols], in0=w_in[("q", j)][:, cols].bitcast(FP8),
                                     in1=scale_bc[:, cols], op=ALU.mult)
+
+        def cast(j):
+            if SPASS:
+                nc.scalar.copy(out=st[("wbf", j)][:, v_cols:HID], in_=w_in[("q", j)][:, v_cols:HID].bitcast(FP8))
 
         def stage_t(u):
             kind, h = units[u]
@@ -190,11 +194,21 @@ def tile_densemha_pa_kernel(tc, hidden_states, Wq_bytes, Wq_scale, bq, Wk, bk, o
             st[("tp", u)] = banks
 
         def stage_e(u):
+            kind, h = units[u]
             wg = work.tile([P, HID], BF16, name="wg", tag="wg", bufs=3, align_bytes=64)
             wgw = wg[:].bitcast(F32)
             for j in range(2):
-                nc.scalar.copy(out=wgw[:, 512 * j:512 * (j + 1)].rearrange("p (g r e) -> p g r e", g=2, e=2),
-                               in_=st[("tp", u)][j][:].rearrange("p (g e r) -> p g r e", g=2, e=2))
+                bank = st[("tp", u)][j]
+                n_g = 2 if kind != "q" or j == 0 else 2 - SPASS
+                if n_g:
+                    nc.scalar.copy(out=wgw[:, 512 * j:512 * j + 256 * n_g].rearrange("p (g r e) -> p g r e", g=n_g, e=2),
+                                   in_=bank[:, 0:256 * n_g].rearrange("p (g e r) -> p g r e", g=n_g, e=2))
+                for gl in range(n_g, 2):
+                    g = 2 * j + gl
+                    for t in range(4):
+                        i0 = 512 * gl + 256 * (t // 2) + t % 2
+                        nc.scalar.activation(out=wg[:, 512 * g + t:512 * (g + 1):4], in_=bank[:].bitcast(BF16)[:, i0:i0 + 256 - t % 2:2],
+                                             func=ACT.Copy, scale=s_t[:, 4 * g + t:4 * g + t + 1])
             st[("wg", u)] = wg
 
         def stage_q(u):
@@ -252,30 +266,33 @@ def tile_densemha_pa_kernel(tc, hidden_states, Wq_bytes, Wq_scale, bq, Wk, bk, o
             nc.scalar.dma_start(out=dst[0, h].rearrange("(p a) d -> p (a d)", a=4), in_=ob[:])
 
         widen_at = {}
-        for u in range(n_units):
-            kind, h = units[u]
-            if kind == "q":
-                lead = 3 if h < HEADS - 1 else 2
-                widen_at[u - lead] = (h, 0)
-                widen_at[u - lead + 1] = (h, 1)
+        step = n_units
+        for h in reversed(range(HEADS)):
+            for half in (1, 0):
+                step = min(step - 1, units.index(("q", h)) - 2)
+                widen_at.setdefault(max(step, W_FIRST + (2 * h + half) // 2), []).append((h, half))
 
         def is_head(u):
             return n_x <= u < n_units
 
         for u in range(n_units + LAG_F):
-            if u == 0:
-                spread_transposes(0)
-                spread_out(0, True)
-                spread_out(1, False)
-            if u == 1:
-                spread_transposes(1)
-                spread_out(2, False)
-                spread_out(3, False)
             if u < n_units:
                 stage_t(u)
                 stage_e(u)
+            if u == 3:
+                bias_columns()
+            if u == 5:
+                tables()
+            if u in (4, 5):
+                spread_transposes(u - 4)
             if 0 <= u - LAG_Q < n_units:
                 stage_q(u - LAG_Q)
+            if u == 4:
+                spread_out(0, False)
+                spread_out(1, False)
+            if u == 5:
+                spread_out(2, True)
+                spread_out(3, True)
             if is_head(u - LAG_F):
                 stage_f(u - LAG_F)
                 stage_o(u - LAG_F)
@@ -283,10 +300,7 @@ def tile_densemha_pa_kernel(tc, hidden_states, Wq_bytes, Wq_scale, bq, Wk, bk, o
                 stage_m(u - LAG_M)
             if is_head(u - LAG_Z):
                 stage_z(u - LAG_Z)
-            if u in widen_at:
-                widen(widen_at[u][0], widen_at[u][1])
-            if u == 1:
-                table_cos()
-            if u == 2:
-                table_sin()
-                bias_columns()
+            for j, half in reversed(widen_at.get(u, [])):
+                widen(j, half)
+                if half == 0:
+                    cast(j)

@@ -26,11 +26,22 @@ LAG_Q = 1
 LAG_M = 1
 LAG_Z = 2
 LAG_F = 3
-AHEAD = 2
-W_FIRST = 5
-SPASS = 1
+AHEAD = 1
+SP = 2
+W_FIRST = 4
+SHARED = (1, 3, 5, 7, 9, 11, 13)
+SCALE_DMA = False
+BC_AFTER = ("k", 0)
+EV_SCALAR = (2, 3)
+T_TABLES = 5
+T_BIAS = 3
+W_WHOLE = False
 
 TWO_PI = 2.0 * math.pi
+
+
+def LOADS(units):
+    return units
 
 
 def tile_densemha_pa_kernel(tc, hidden_states, Wq_bytes, Wq_scale, bq, Wk, bk, out_0, out_1):
@@ -49,18 +60,18 @@ def tile_densemha_pa_kernel(tc, hidden_states, Wq_bytes, Wq_scale, bq, Wk, bk, o
         n_x = 4
         units = [("x", a) for a in range(n_x)] + seq
         n_units = len(units)
-        v_cols = HID - 512 * SPASS
 
         x_view = hidden_states[0].rearrange("(p a) k -> a p k", a=4)
         x_sb = []
-        sc_rows = const.tile([P, P], F32, name="sc_rows", tag="sc_rows")
-        nc.gpsimd.memset(sc_rows[:], 0.0)
-        nc.sync.dma_start(out=sc_rows[0:16, :], in_=Wq_scale.rearrange("o (c p) -> (o c) p", p=P))
+        if not SCALE_DMA:
+            sc_rows = const.tile([P, P], F32, name="sc_rows", tag="sc_rows")
+            nc.gpsimd.memset(sc_rows[:], 0.0)
+            nc.sync.dma_start(out=sc_rows[0:16, :], in_=Wq_scale.rearrange("o (c p) -> (o c) p", p=P))
         scale_bc = const.tile([P, HID], F32, name="scale_bc", tag="scale_bc")
         wq_view = Wq_bytes.rearrange("(h n) k -> h n k", n=P)
         wk_view = Wk.rearrange("(h n) k -> h n k", n=P)
         w_in = {}
-        for kind, h in units:
+        for kind, h in LOADS(units):
             if kind == "x":
                 wt = const.tile([P, HID], BF16, name="x_sb%d" % h, tag="x_sb%d" % h)
                 nc.sync.dma_start(out=wt[:], in_=x_view[h])
@@ -73,6 +84,8 @@ def tile_densemha_pa_kernel(tc, hidden_states, Wq_bytes, Wq_scale, bq, Wk, bk, o
                 wt = const.tile([P, HID], BF16, name="wk_sb%d" % h, tag="wk_sb%d" % h)
                 nc.sync.dma_start(out=wt[:], in_=wk_view[h])
                 w_in[(kind, h)] = wt
+            if SCALE_DMA and (kind, h) == BC_AFTER:
+                nc.sync.dma_start(out=scale_bc[:], in_=Wq_scale.rearrange("o k -> (o k)").partition_broadcast(P))
 
         dmy = const.tile([P, 1], F32, name="dmy", tag="dmy")
         dmy2 = const.tile([P, 1], F32, name="dmy2", tag="dmy2")
@@ -102,10 +115,11 @@ def tile_densemha_pa_kernel(tc, hidden_states, Wq_bytes, Wq_scale, bq, Wk, bk, o
         nc.tensor.transpose(out=thp[:, 0:P], in_=th[:], identity=ident[:])
         thc = const.tile([P, 1], F32, name="thc", tag="thc")
         nc.vector.tensor_copy(out=thc[:], in_=thp[:, 0:1])
-        scp = psum.tile([P, 512], F32, name="scp", tag="acc", bufs=2)
-        nc.tensor.transpose(out=scp[:, 0:P], in_=sc_rows[:], identity=ident[:])
         s_col = const.tile([P, 16], F32, name="s_col", tag="s_col")
-        nc.vector.tensor_copy(out=s_col[:], in_=scp[:, 0:16])
+        if not SCALE_DMA:
+            scp = psum.tile([P, 512], F32, name="scp", tag="acc", bufs=2)
+            nc.tensor.transpose(out=scp[:, 0:P], in_=sc_rows[:], identity=ident[:])
+            nc.vector.tensor_copy(out=s_col[:], in_=scp[:, 0:16])
         perm = const.tile([P, P], F32, name="perm", tag="perm")
         bbf = const.tile([P, P], F32, name="bbf", tag="bbf")
         bias = const.tile([P, 2 * HEADS], F32, name="bias", tag="bias")
@@ -164,13 +178,18 @@ def tile_densemha_pa_kernel(tc, hidden_states, Wq_bytes, Wq_scale, bq, Wk, bk, o
         def widen(j, half):
             if half == 0:
                 st[("wbf", j)] = work.tile([P, HID], BF16, name="wbf", tag="wbf", bufs=4)
+            v_cols = HID - 512 * (j in SHARED)
             cols = slice(half * v_cols // 2, (half + 1) * v_cols // 2)
+            if W_WHOLE:
+                if half == 0:
+                    return
+                cols = slice(0, v_cols)
             nc.vector.tensor_tensor(out=st[("wbf", j)][:, cols], in0=w_in[("q", j)][:, cols].bitcast(FP8),
                                     in1=scale_bc[:, cols], op=ALU.mult)
 
         def cast(j):
-            if SPASS:
-                nc.scalar.copy(out=st[("wbf", j)][:, v_cols:HID], in_=w_in[("q", j)][:, v_cols:HID].bitcast(FP8))
+            if j in SHARED:
+                nc.scalar.copy(out=st[("wbf", j)][:, 1536:HID], in_=w_in[("q", j)][:, 1536:HID].bitcast(FP8))
 
         def stage_t(u):
             kind, h = units[u]
@@ -199,7 +218,7 @@ def tile_densemha_pa_kernel(tc, hidden_states, Wq_bytes, Wq_scale, bq, Wk, bk, o
             wgw = wg[:].bitcast(F32)
             for j in range(2):
                 bank = st[("tp", u)][j]
-                n_g = 2 if kind != "q" or j == 0 else 2 - SPASS
+                n_g = 1 if kind == "q" and j == 1 and h in SHARED else 2
                 if n_g:
                     nc.scalar.copy(out=wgw[:, 512 * j:512 * j + 256 * n_g].rearrange("p (g r e) -> p g r e", g=n_g, e=2),
                                    in_=bank[:, 0:256 * n_g].rearrange("p (g e r) -> p g r e", g=n_g, e=2))
@@ -279,20 +298,17 @@ def tile_densemha_pa_kernel(tc, hidden_states, Wq_bytes, Wq_scale, bq, Wk, bk, o
             if u < n_units:
                 stage_t(u)
                 stage_e(u)
-            if u == 3:
+            if u == T_BIAS:
                 bias_columns()
-            if u == 5:
+            if u == T_TABLES:
                 tables()
-            if u in (4, 5):
-                spread_transposes(u - 4)
+            if not SCALE_DMA and u in (SP, SP + 1):
+                spread_transposes(u - SP)
             if 0 <= u - LAG_Q < n_units:
                 stage_q(u - LAG_Q)
-            if u == 4:
-                spread_out(0, False)
-                spread_out(1, False)
-            if u == 5:
-                spread_out(2, True)
-                spread_out(3, True)
+            if not SCALE_DMA and u in (SP, SP + 1):
+                for b in (2 * (u - SP), 2 * (u - SP) + 1):
+                    spread_out(b, b in EV_SCALAR)
             if is_head(u - LAG_F):
                 stage_f(u - LAG_F)
                 stage_o(u - LAG_F)

@@ -27,15 +27,19 @@ LAG_M = 1
 LAG_Z = 2
 LAG_F = 3
 AHEAD = 1
-SP = 2
+SP = (1, 3)
+E_VEC = ()
 W_FIRST = 4
-SHARED = (1, 3, 5, 7, 9, 11, 13)
+SHARED = ()
 SCALE_DMA = False
 BC_AFTER = ("k", 0)
 EV_SCALAR = (2, 3)
 T_TABLES = 5
 T_BIAS = 3
 W_WHOLE = False
+RUNS = tuple(range(2, 16))
+RO_LEAD = 3
+RO_POS = 1
 
 TWO_PI = 2.0 * math.pi
 
@@ -200,6 +204,8 @@ def tile_densemha_pa_kernel(tc, hidden_states, Wq_bytes, Wq_scale, bq, Wk, bk, o
             else:
                 src = st[("wbf", h)]
             words = src[:].bitcast(F32)
+            if kind == "k" and h in RUNS:
+                words = st[("runs", h)][:]
             banks = []
             for j in range(2):
                 bank = psum.tile([P, 512], F32, name="tp", tag="tp", bufs=4)
@@ -207,10 +213,18 @@ def tile_densemha_pa_kernel(tc, hidden_states, Wq_bytes, Wq_scale, bq, Wk, bk, o
                     g = 2 * j + gl
                     for e in range(2):
                         c0 = (2 * gl + e) * P
-                        nc.tensor.transpose(out=bank[:, c0:c0 + P], in_=words[:, 256 * g + e:256 * (g + 1):2],
-                                            identity=ident[:])
+                        in_words = words[:, 256 * g + e:256 * (g + 1):2]
+                        if kind == "k" and h in RUNS:
+                            in_words = words[:, 256 * g + P * e:256 * g + P * (e + 1)]
+                        nc.tensor.transpose(out=bank[:, c0:c0 + P], in_=in_words, identity=ident[:])
                 banks.append(bank)
             st[("tp", u)] = banks
+
+        def reorder(h):
+            rt = work.tile([P, HID // 2], F32, name="runs", tag="runs", bufs=3)
+            nc.scalar.copy(out=rt[:].rearrange("p (g e q) -> p g e q", g=PASSES, e=2),
+                           in_=w_in[("k", h)][:].bitcast(F32).rearrange("p (g q e) -> p g e q", g=PASSES, e=2))
+            st[("runs", h)] = rt
 
         def stage_e(u):
             kind, h = units[u]
@@ -220,7 +234,8 @@ def tile_densemha_pa_kernel(tc, hidden_states, Wq_bytes, Wq_scale, bq, Wk, bk, o
                 bank = st[("tp", u)][j]
                 n_g = 1 if kind == "q" and j == 1 and h in SHARED else 2
                 if n_g:
-                    nc.scalar.copy(out=wgw[:, 512 * j:512 * j + 256 * n_g].rearrange("p (g r e) -> p g r e", g=n_g, e=2),
+                    copy = nc.vector.tensor_copy if (u, j) in E_VEC else nc.scalar.copy
+                    copy(out=wgw[:, 512 * j:512 * j + 256 * n_g].rearrange("p (g r e) -> p g r e", g=n_g, e=2),
                                    in_=bank[:, 0:256 * n_g].rearrange("p (g e r) -> p g r e", g=n_g, e=2))
                 for gl in range(n_g, 2):
                     g = 2 * j + gl
@@ -295,20 +310,27 @@ def tile_densemha_pa_kernel(tc, hidden_states, Wq_bytes, Wq_scale, bq, Wk, bk, o
             return n_x <= u < n_units
 
         for u in range(n_units + LAG_F):
+            ro = u + RO_LEAD
+            if RO_POS == 0 and ro < n_units and units[ro][0] == "k" and units[ro][1] in RUNS:
+                reorder(units[ro][1])
             if u < n_units:
                 stage_t(u)
                 stage_e(u)
+            if RO_POS == 1 and ro < n_units and units[ro][0] == "k" and units[ro][1] in RUNS:
+                reorder(units[ro][1])
             if u == T_BIAS:
                 bias_columns()
             if u == T_TABLES:
                 tables()
-            if not SCALE_DMA and u in (SP, SP + 1):
-                spread_transposes(u - SP)
+            for half in (0, 1):
+                if not SCALE_DMA and u == SP[half]:
+                    spread_transposes(half)
             if 0 <= u - LAG_Q < n_units:
                 stage_q(u - LAG_Q)
-            if not SCALE_DMA and u in (SP, SP + 1):
-                for b in (2 * (u - SP), 2 * (u - SP) + 1):
-                    spread_out(b, b in EV_SCALAR)
+            for half in (0, 1):
+                if not SCALE_DMA and u == SP[half]:
+                    for b in (2 * half, 2 * half + 1):
+                        spread_out(b, b in EV_SCALAR)
             if is_head(u - LAG_F):
                 stage_f(u - LAG_F)
                 stage_o(u - LAG_F)

@@ -23,9 +23,12 @@ PASSES = 4
 FLOPS = 2 * 2 * TOK * HID * HID
 
 LAG_Q = 1
-LAG_M = 1
-LAG_Z = 2
-LAG_F = 3
+PAIR_Q = True
+PAIR_FROM = 7
+PAR = 1
+LAG_M = 2
+LAG_Z = 3
+LAG_F = 4
 AHEAD = 1
 SP = (1, 3)
 E_VEC = ()
@@ -39,6 +42,7 @@ T_BIAS = 3
 W_WHOLE = False
 RUNS = tuple(range(2, 16))
 RO_LEAD = 3
+RUNS_Q = ()
 RO_POS = 1
 
 TWO_PI = 2.0 * math.pi
@@ -206,6 +210,8 @@ def tile_densemha_pa_kernel(tc, hidden_states, Wq_bytes, Wq_scale, bq, Wk, bk, o
             words = src[:].bitcast(F32)
             if kind == "k" and h in RUNS:
                 words = st[("runs", h)][:]
+            if kind == "q" and h in RUNS_Q:
+                words = st[("runsq", h)][:]
             banks = []
             for j in range(2):
                 bank = psum.tile([P, 512], F32, name="tp", tag="tp", bufs=4)
@@ -214,11 +220,17 @@ def tile_densemha_pa_kernel(tc, hidden_states, Wq_bytes, Wq_scale, bq, Wk, bk, o
                     for e in range(2):
                         c0 = (2 * gl + e) * P
                         in_words = words[:, 256 * g + e:256 * (g + 1):2]
-                        if kind == "k" and h in RUNS:
+                        if (kind == "k" and h in RUNS) or (kind == "q" and h in RUNS_Q):
                             in_words = words[:, 256 * g + P * e:256 * g + P * (e + 1)]
                         nc.tensor.transpose(out=bank[:, c0:c0 + P], in_=in_words, identity=ident[:])
                 banks.append(bank)
             st[("tp", u)] = banks
+
+        def reorder_q(h):
+            rt = work.tile([P, HID // 2], F32, name="runs", tag="runs", bufs=3)
+            nc.scalar.copy(out=rt[:].rearrange("p (g e q) -> p g e q", g=PASSES, e=2),
+                           in_=st[("wbf", h)][:].bitcast(F32).rearrange("p (g q e) -> p g e q", g=PASSES, e=2))
+            st[("runsq", h)] = rt
 
         def reorder(h):
             rt = work.tile([P, HID // 2], F32, name="runs", tag="runs", bufs=3)
@@ -228,7 +240,7 @@ def tile_densemha_pa_kernel(tc, hidden_states, Wq_bytes, Wq_scale, bq, Wk, bk, o
 
         def stage_e(u):
             kind, h = units[u]
-            wg = work.tile([P, HID], BF16, name="wg", tag="wg", bufs=3, align_bytes=64)
+            wg = work.tile([P, HID], BF16, name="wg", tag="wg", bufs=5, align_bytes=64)
             wgw = wg[:].bitcast(F32)
             for j in range(2):
                 bank = st[("tp", u)][j]
@@ -254,8 +266,8 @@ def tile_densemha_pa_kernel(tc, hidden_states, Wq_bytes, Wq_scale, bq, Wk, bk, o
                                           scales=xs[g][:, h * P:(h + 1) * P],
                                           in_=wg[:, g * 512:(g + 1) * 512])
             else:
-                wc = work.tile([P, 512], U32, name="wc", tag="wc", bufs=3, align_bytes=64)
-                ws = work.tile([P, 512], U8, name="ws", tag="ws", bufs=3, align_bytes=64)
+                wc = work.tile([P, 512], U32, name="wc", tag="wc", bufs=5, align_bytes=64)
+                ws = work.tile([P, 512], U8, name="ws", tag="ws", bufs=5, align_bytes=64)
                 nc.vector.quantize_mx(out=wc[:].bitcast(FP8X4), scales=ws[:], in_=wg[:])
                 st[("wc", u)] = (wc, ws)
 
@@ -273,8 +285,8 @@ def tile_densemha_pa_kernel(tc, hidden_states, Wq_bytes, Wq_scale, bq, Wk, bk, o
             kind, h = units[u]
             col = h if kind == "q" else HEADS + h
             acc = st[("acc", u)]
-            z1 = work.tile([P, TOK], F32, name="z1", tag="z1", bufs=3)
-            z2 = work.tile([P, TOK], F32, name="z2", tag="z2", bufs=3)
+            z1 = work.tile([P, TOK], F32, name="z1", tag="z1", bufs=4)
+            z2 = work.tile([P, TOK], F32, name="z2", tag="z2", bufs=4)
             nc.vector.scalar_tensor_tensor(out=z1[:], in0=acc[:], scalar=bias[:, col:col + 1], in1=cos_t[:],
                                            op0=ALU.add, op1=ALU.mult)
             nc.vector.scalar_tensor_tensor(out=z2[:], in0=acc[:], scalar=bias[:, col:col + 1], in1=sin_t[:],
@@ -318,6 +330,9 @@ def tile_densemha_pa_kernel(tc, hidden_states, Wq_bytes, Wq_scale, bq, Wk, bk, o
                 stage_e(u)
             if RO_POS == 1 and ro < n_units and units[ro][0] == "k" and units[ro][1] in RUNS:
                 reorder(units[ro][1])
+            rq = u + 1
+            if rq < n_units and units[rq][0] == "q" and units[rq][1] in RUNS_Q:
+                reorder_q(units[rq][1])
             if u == T_BIAS:
                 bias_columns()
             if u == T_TABLES:
@@ -325,7 +340,8 @@ def tile_densemha_pa_kernel(tc, hidden_states, Wq_bytes, Wq_scale, bq, Wk, bk, o
             for half in (0, 1):
                 if not SCALE_DMA and u == SP[half]:
                     spread_transposes(half)
-            if 0 <= u - LAG_Q < n_units:
+            q_last = PAIR_Q and u >= PAIR_FROM and u % 2 == PAR and u < n_units
+            if 0 <= u - LAG_Q < n_units and not q_last:
                 stage_q(u - LAG_Q)
             for half in (0, 1):
                 if not SCALE_DMA and u == SP[half]:
@@ -342,3 +358,5 @@ def tile_densemha_pa_kernel(tc, hidden_states, Wq_bytes, Wq_scale, bq, Wk, bk, o
                 widen(j, half)
                 if half == 0:
                     cast(j)
+            if q_last:
+                stage_q(u - LAG_Q)

@@ -232,15 +232,16 @@ def tile_densemha_pa_kernel(tc, hidden_states, Wq_bytes, Wq_scale, bq, Wk, bk, o
                            in_=st[("wbf", h)][:].bitcast(F32).rearrange("p (g q e) -> p g e q", g=PASSES, e=2))
             st[("runsq", h)] = rt
 
-        def reorder(h):
-            rt = work.tile([P, HID // 2], F32, name="runs", tag="runs", bufs=3)
-            nc.scalar.copy(out=rt[:].rearrange("p (g e q) -> p g e q", g=PASSES, e=2),
-                           in_=w_in[("k", h)][:].bitcast(F32).rearrange("p (g q e) -> p g e q", g=PASSES, e=2))
-            st[("runs", h)] = rt
+        def reorder(h, half):
+            if half == 0:
+                st[("runs", h)] = work.tile([P, HID // 2], F32, name="runs", tag="runs", bufs=3)
+            cols = slice(512 * half, 512 * (half + 1))
+            nc.scalar.copy(out=st[("runs", h)][:, cols].rearrange("p (g e q) -> p g e q", g=2, e=2),
+                           in_=w_in[("k", h)][:].bitcast(F32)[:, cols].rearrange("p (g q e) -> p g e q", g=2, e=2))
 
         def stage_e(u):
             kind, h = units[u]
-            wg = work.tile([P, HID], BF16, name="wg", tag="wg", bufs=5, align_bytes=64)
+            wg = work.tile([P, HID], BF16, name="wg", tag="wg", bufs=4, align_bytes=64)
             wgw = wg[:].bitcast(F32)
             for j in range(2):
                 bank = st[("tp", u)][j]
@@ -307,9 +308,9 @@ def tile_densemha_pa_kernel(tc, hidden_states, Wq_bytes, Wq_scale, bq, Wk, bk, o
         def stage_o(u):
             kind, h = units[u]
             dst = out_0 if kind == "q" else out_1
-            ob = work.tile([P, TOK], F32, name="ob", tag="ob", bufs=4)
+            ob = work.tile([P, TOK], F32, name="ob", tag="ob", bufs=6)
             nc.scalar.copy(out=ob[:], in_=st[("fin", u)][:])
-            nc.scalar.dma_start(out=dst[0, h].rearrange("(p a) d -> p (a d)", a=4), in_=ob[:])
+            nc.sync.dma_start(out=dst[0, h].rearrange("(p a) d -> p (a d)", a=4), in_=ob[:])
 
         widen_at = {}
         step = n_units
@@ -322,17 +323,13 @@ def tile_densemha_pa_kernel(tc, hidden_states, Wq_bytes, Wq_scale, bq, Wk, bk, o
             return n_x <= u < n_units
 
         for u in range(n_units + LAG_F):
-            ro = u + RO_LEAD
-            if RO_POS == 0 and ro < n_units and units[ro][0] == "k" and units[ro][1] in RUNS:
-                reorder(units[ro][1])
             if u < n_units:
                 stage_t(u)
                 stage_e(u)
-            if RO_POS == 1 and ro < n_units and units[ro][0] == "k" and units[ro][1] in RUNS:
-                reorder(units[ro][1])
-            rq = u + 1
-            if rq < n_units and units[rq][0] == "q" and units[rq][1] in RUNS_Q:
-                reorder_q(units[rq][1])
+            for half in (0, 1):
+                ro = u + RO_LEAD - half
+                if ro < n_units and units[ro][0] == "k" and units[ro][1] in RUNS:
+                    reorder(units[ro][1], half)
             if u == T_BIAS:
                 bias_columns()
             if u == T_TABLES:

@@ -22,10 +22,12 @@ DH = 128
 PASSES = 4
 FLOPS = 2 * 2 * TOK * HID * HID
 
-LAG_Q = 1
+RAMP = 2
+LQ = 1
+QE = 0
 PAIR_Q = True
 PAIR_FROM = 7
-PAR = 1
+PAR = 0
 LAG_M = 2
 LAG_Z = 3
 LAG_F = 4
@@ -33,7 +35,7 @@ AHEAD = 1
 SP = (1, 3)
 E_VEC = ()
 W_FIRST = 4
-SHARED = ()
+SHARED = (3, 6, 9, 12)
 SCALE_DMA = False
 BC_AFTER = ("k", 0)
 EV_SCALAR = (2, 3)
@@ -267,50 +269,61 @@ def tile_densemha_pa_kernel(tc, hidden_states, Wq_bytes, Wq_scale, bq, Wk, bk, o
                                           scales=xs[g][:, h * P:(h + 1) * P],
                                           in_=wg[:, g * 512:(g + 1) * 512])
             else:
-                wc = work.tile([P, 512], U32, name="wc", tag="wc", bufs=5, align_bytes=64)
-                ws = work.tile([P, 512], U8, name="ws", tag="ws", bufs=5, align_bytes=64)
+                wc = work.tile([P, 512], U32, name="wc", tag="wc", bufs=4, align_bytes=64)
+                ws = work.tile([P, 512], U8, name="ws", tag="ws", bufs=4, align_bytes=64)
                 nc.vector.quantize_mx(out=wc[:].bitcast(FP8X4), scales=ws[:], in_=wg[:])
                 st[("wc", u)] = (wc, ws)
 
+        def token_parts(u):
+            n = 2 if u == n_units - 1 else 1
+            return [slice(i * TOK // n, (i + 1) * TOK // n) for i in range(n)]
+
         def stage_m(u):
             wc, ws = st[("wc", u)]
-            acc = psum.tile([P, 512], F32, name="acc", tag="acc", bufs=2)
-            for g in range(PASSES):
-                nc.tensor.matmul_mx(out=acc[:], lhsT=wc[:, g * P:(g + 1) * P].bitcast(FP8X4),
-                                    lhsT_scale=ws[:, g * P:(g + 1) * P],
-                                    rhs=xc[g][:].bitcast(FP8X4), rhs_scale=xs[g][:],
-                                    start=(g == 0), stop=(g == PASSES - 1))
-            st[("acc", u)] = acc
+            for cols in token_parts(u):
+                acc = psum.tile([P, 512], F32, name="acc", tag="acc", bufs=2)
+                for g in range(PASSES):
+                    nc.tensor.matmul_mx(out=acc[:, cols], lhsT=wc[:, g * P:(g + 1) * P].bitcast(FP8X4),
+                                        lhsT_scale=ws[:, g * P:(g + 1) * P],
+                                        rhs=xc[g][:, cols].bitcast(FP8X4), rhs_scale=xs[g][:, cols],
+                                        start=(g == 0), stop=(g == PASSES - 1))
+                st[("acc", u, cols.start)] = acc
 
         def stage_z(u):
             kind, h = units[u]
             col = h if kind == "q" else HEADS + h
-            acc = st[("acc", u)]
             z1 = work.tile([P, TOK], F32, name="z1", tag="z1", bufs=4)
             z2 = work.tile([P, TOK], F32, name="z2", tag="z2", bufs=4)
-            nc.vector.scalar_tensor_tensor(out=z1[:], in0=acc[:], scalar=bias[:, col:col + 1], in1=cos_t[:],
-                                           op0=ALU.add, op1=ALU.mult)
-            nc.vector.scalar_tensor_tensor(out=z2[:], in0=acc[:], scalar=bias[:, col:col + 1], in1=sin_t[:],
-                                           op0=ALU.add, op1=ALU.mult)
+            for cols in token_parts(u):
+                acc = st[("acc", u, cols.start)]
+                for z, table in ((z1, cos_t), (z2, sin_t)):
+                    nc.vector.scalar_tensor_tensor(out=z[:, cols], in0=acc[:, cols], scalar=bias[:, col:col + 1],
+                                                   in1=table[:, cols], op0=ALU.add, op1=ALU.mult)
             st[("z", u)] = (z1, z2)
 
         def stage_f(u):
             z1, z2 = st[("z", u)]
-            fin = psum.tile([P, 512], F32, name="fin", tag="fin", bufs=2)
-            for a in range(4):
-                cols = slice(a * P, (a + 1) * P)
-                nc.tensor.matmul(out=fin[:, cols], lhsT=z1[:, cols], rhs=ident[:], is_transpose=True,
-                                 start=True, stop=False)
-                nc.tensor.matmul(out=fin[:, cols], lhsT=z2[:, cols], rhs=perm[:], is_transpose=True,
-                                 start=False, stop=True)
-            st[("fin", u)] = fin
+            for part in token_parts(u):
+                if u == n_units - 1:
+                    fin = psum.tile([P, 512], F32, name="fin", tag="tp", bufs=4)
+                else:
+                    fin = psum.tile([P, 512], F32, name="fin", tag="fin", bufs=2)
+                for c0 in range(part.start, part.stop, P):
+                    cols = slice(c0, c0 + P)
+                    nc.tensor.matmul(out=fin[:, cols], lhsT=z1[:, cols], rhs=ident[:], is_transpose=True,
+                                     start=True, stop=False)
+                    nc.tensor.matmul(out=fin[:, cols], lhsT=z2[:, cols], rhs=perm[:], is_transpose=True,
+                                     start=False, stop=True)
+                st[("fin", u, part.start)] = fin
 
         def stage_o(u):
             kind, h = units[u]
             dst = out_0 if kind == "q" else out_1
             ob = work.tile([P, TOK], F32, name="ob", tag="ob", bufs=6)
-            nc.scalar.copy(out=ob[:], in_=st[("fin", u)][:])
-            nc.sync.dma_start(out=dst[0, h].rearrange("(p a) d -> p (a d)", a=4), in_=ob[:])
+            for part in token_parts(u):
+                nc.scalar.copy(out=ob[:, part], in_=st[("fin", u, part.start)][:, part])
+                queue = nc.sync if part.start == 0 else nc.scalar
+                queue.dma_start(out=dst[0, h].rearrange("(p a) d -> p (a d)", a=4)[:, part], in_=ob[:, part])
 
         widen_at = {}
         step = n_units
@@ -322,7 +335,18 @@ def tile_densemha_pa_kernel(tc, hidden_states, Wq_bytes, Wq_scale, bq, Wk, bk, o
         def is_head(u):
             return n_x <= u < n_units
 
-        for u in range(n_units + LAG_F):
+        q_at, m_at, z_at, f_at = {}, {}, {}, {}
+        for u in range(n_units):
+            q_at[u] = u + 1 if u < n_x + RAMP else min(u + LQ, n_units + QE)
+            if u >= n_x:
+                m_at[u] = max(q_at[u] + 1, m_at.get(u - 1, 0) + (1 if u < n_units - 1 else 1))
+                z_at[u] = m_at[u] + 1
+                f_at[u] = z_at[u] + 1
+
+        def due(at, s):
+            return [u for u in sorted(at) if at[u] == s]
+
+        for u in range(f_at[n_units - 1] + 1):
             if u < n_units:
                 stage_t(u)
                 stage_e(u)
@@ -335,25 +359,31 @@ def tile_densemha_pa_kernel(tc, hidden_states, Wq_bytes, Wq_scale, bq, Wk, bk, o
             if u == T_TABLES:
                 tables()
             for half in (0, 1):
-                if not SCALE_DMA and u == SP[half]:
+                if u == SP[half]:
                     spread_transposes(half)
-            q_last = PAIR_Q and u >= PAIR_FROM and u % 2 == PAR and u < n_units
-            if 0 <= u - LAG_Q < n_units and not q_last:
-                stage_q(u - LAG_Q)
+            q_last = u >= PAIR_FROM and u % 2 == PAR and u < n_units
+            if not q_last:
+                for v in due(q_at, u):
+                    stage_q(v)
             for half in (0, 1):
-                if not SCALE_DMA and u == SP[half]:
+                if u == SP[half]:
                     for b in (2 * half, 2 * half + 1):
                         spread_out(b, b in EV_SCALAR)
-            if is_head(u - LAG_F):
-                stage_f(u - LAG_F)
-                stage_o(u - LAG_F)
-            if is_head(u - LAG_M):
-                stage_m(u - LAG_M)
-            if is_head(u - LAG_Z):
-                stage_z(u - LAG_Z)
+            if u >= n_units:
+                for v in due(m_at, u):
+                    stage_m(v)
+            for v in due(f_at, u):
+                stage_f(v)
+                stage_o(v)
+            if u < n_units:
+                for v in due(m_at, u):
+                    stage_m(v)
+            for v in due(z_at, u):
+                stage_z(v)
             for j, half in reversed(widen_at.get(u, [])):
                 widen(j, half)
                 if half == 0:
                     cast(j)
             if q_last:
-                stage_q(u - LAG_Q)
+                for v in due(q_at, u):
+                    stage_q(v)

import math
from contextlib import ExitStack

import concourse.mybir as mybir
from concourse.masks import make_identity

F32 = mybir.dt.float32
BF16 = mybir.dt.bfloat16
U32 = mybir.dt.uint32
U8 = mybir.dt.uint8
I32 = mybir.dt.int32
FP8 = mybir.dt.float8_e4m3fn
FP8X4 = mybir.dt.float8_e4m3fn_x4
ALU = mybir.AluOpType
ACT = mybir.ActivationFunctionType

P = 128
TOK = 512
HID = 2048
HEADS = 16
DH = 128
PASSES = 4
FLOPS = 2 * 2 * TOK * HID * HID

RAMP = 2
LQ = 1
QE = 0
PAIR_Q = True
PAIR_FROM = 7
PAR = 0
LAG_M = 2
LAG_Z = 3
LAG_F = 4
AHEAD = 1
SP = (1, 3)
E_VEC = ()
W_FIRST = 4
SHARED = (3, 6, 9, 12)
SCALE_DMA = False
BC_AFTER = ("k", 0)
EV_SCALAR = (2, 3)
T_TABLES = 5
T_BIAS = 3
W_WHOLE = False
RUNS = tuple(range(2, 16))
RO_LEAD = 3
RUNS_Q = ()
RO_POS = 1

TWO_PI = 2.0 * math.pi


def LOADS(units):
    return units


def tile_densemha_pa_kernel(tc, hidden_states, Wq_bytes, Wq_scale, bq, Wk, bk, out_0, out_1):
    nc = tc.nc
    with ExitStack() as ctx:
        const = ctx.enter_context(tc.tile_pool(name="const", bufs=1))
        work = ctx.enter_context(tc.tile_pool(name="work", bufs=3))
        psum = ctx.enter_context(tc.psum_pool(name="psum", bufs=2))
        ctx.enter_context(tc.manual_schedule())

        seq = [("k", h) for h in range(AHEAD)]
        for j in range(HEADS - AHEAD):
            seq.append(("q", j))
            seq.append(("k", j + AHEAD))
        seq += [("q", h) for h in range(HEADS - AHEAD, HEADS)]
        n_x = 4
        units = [("x", a) for a in range(n_x)] + seq
        n_units = len(units)

        x_view = hidden_states[0].rearrange("(p a) k -> a p k", a=4)
        x_sb = []
        if not SCALE_DMA:
            sc_rows = const.tile([P, P], F32, name="sc_rows", tag="sc_rows")
            nc.gpsimd.memset(sc_rows[:], 0.0)
            nc.sync.dma_start(out=sc_rows[0:16, :], in_=Wq_scale.rearrange("o (c p) -> (o c) p", p=P))
        scale_bc = const.tile([P, HID], F32, name="scale_bc", tag="scale_bc")
        wq_view = Wq_bytes.rearrange("(h n) k -> h n k", n=P)
        wk_view = Wk.rearrange("(h n) k -> h n k", n=P)
        w_in = {}
        for kind, h in LOADS(units):
            if kind == "x":
                wt = const.tile([P, HID], BF16, name="x_sb%d" % h, tag="x_sb%d" % h)
                nc.sync.dma_start(out=wt[:], in_=x_view[h])
                x_sb.append(wt)
            elif kind == "q":
                wt = const.tile([P, HID], U8, name="wq_bytes%d" % h, tag="wq_bytes%d" % h)
                nc.sync.dma_start(out=wt[:], in_=wq_view[h])
                w_in[(kind, h)] = wt
            else:
                wt = const.tile([P, HID], BF16, name="wk_sb%d" % h, tag="wk_sb%d" % h)
                nc.sync.dma_start(out=wt[:], in_=wk_view[h])
                w_in[(kind, h)] = wt
            if SCALE_DMA and (kind, h) == BC_AFTER:
                nc.sync.dma_start(out=scale_bc[:], in_=Wq_scale.rearrange("o k -> (o k)").partition_broadcast(P))

        dmy = const.tile([P, 1], F32, name="dmy", tag="dmy")
        dmy2 = const.tile([P, 1], F32, name="dmy2", tag="dmy2")
        nc.gpsimd.memset(dmy[:], 0.0)
        bb = const.tile([P, P], BF16, name="bb", tag="bb")
        nc.vector.memset(bb[:], 0.0)
        s_t = const.tile([P, 16], F32, name="s_t", tag="s_t")
        nc.scalar.dma_start(out=bb[0:HEADS, :], in_=bq.rearrange("(h d) -> h d", d=DH))
        nc.scalar.dma_start(out=bb[HEADS:2 * HEADS, :], in_=bk.rearrange("(h d) -> h d", d=DH))
        nc.scalar.dma_start(out=s_t[:].rearrange("p (g t) -> p g t", t=4),
                            in_=Wq_scale.rearrange("o (g p t) -> p (o g) t", p=P, t=4))
        nc.scalar.activation(out=dmy2[:], in_=dmy[:], func=ACT.Sin)

        ident = const.tile([P, P], F32, name="ident", tag="ident")
        make_identity(nc, ident[:])
        tok = const.tile([P, TOK], F32, name="tok", tag="tok")
        nc.gpsimd.iota(out=tok[:], pattern=[[1, 4], [4, P]], base=0, channel_multiplier=0,
                       allow_small_or_imprecise_dtypes=True)

        th = const.tile([P, P], F32, name="th", tag="th")
        ratio = 10000.0 ** (-1.0 / 64.0)
        nc.vector.memset(th[:, 0:1], 1.0)
        for w in (1, 2, 4, 8, 16, 32):
            nc.vector.tensor_scalar(out=th[:, w:2 * w], in0=th[:, 0:w], scalar1=ratio ** w, scalar2=None, op0=ALU.mult)
        nc.vector.tensor_scalar(out=th[:, 64:128], in0=th[:, 0:64], scalar1=-1.0, scalar2=None, op0=ALU.mult)
        thp = psum.tile([P, 512], F32, name="thp", tag="fin", bufs=2)
        nc.tensor.transpose(out=thp[:, 0:P], in_=th[:], identity=ident[:])
        thc = const.tile([P, 1], F32, name="thc", tag="thc")
        nc.vector.tensor_copy(out=thc[:], in_=thp[:, 0:1])
        s_col = const.tile([P, 16], F32, name="s_col", tag="s_col")
        if not SCALE_DMA:
            scp = psum.tile([P, 512], F32, name="scp", tag="acc", bufs=2)
            nc.tensor.transpose(out=scp[:, 0:P], in_=sc_rows[:], identity=ident[:])
            nc.vector.tensor_copy(out=s_col[:], in_=scp[:, 0:16])
        perm = const.tile([P, P], F32, name="perm", tag="perm")
        bbf = const.tile([P, P], F32, name="bbf", tag="bbf")
        bias = const.tile([P, 2 * HEADS], F32, name="bias", tag="bias")

        turns = const.tile([P, TOK], F32, name="turns", tag="turns")
        n_cos = const.tile([P, TOK], I32, name="n_cos", tag="n_cos")
        n_sin = const.tile([P, TOK], I32, name="n_sin", tag="n_sin")
        rs = const.tile([P, TOK], F32, name="rs", tag="rs")
        rc = const.tile([P, TOK], F32, name="rc", tag="rc")
        sin_t = const.tile([P, TOK], F32, name="sin_t", tag="sin_t")
        cos_t = const.tile([P, TOK], F32, name="cos_t", tag="cos_t")
        nc.vector.tensor_scalar(out=turns[:], in0=tok[:], scalar1=thc[:, 0:1], scalar2=1.0 / TWO_PI,
                                op0=ALU.mult, op1=ALU.mult)
        nc.vector.tensor_copy(out=bbf[:], in_=bb[:])
        nc.vector.tensor_scalar(out=n_cos[:], in0=turns[:], scalar1=0.25, scalar2=None, op0=ALU.add)
        nc.vector.tensor_scalar(out=n_sin[:], in0=turns[:], scalar1=0.0, scalar2=None, op0=ALU.add)
        nc.vector.scalar_tensor_tensor(out=rc[:], in0=n_cos[:], scalar=-1.0, in1=turns[:], op0=ALU.mult, op1=ALU.add)
        nc.vector.scalar_tensor_tensor(out=rs[:], in0=n_sin[:], scalar=-1.0, in1=turns[:], op0=ALU.mult, op1=ALU.add)
        nc.vector.tensor_copy(out=perm[:, 0:64], in_=ident[:, 64:128])
        nc.vector.tensor_copy(out=perm[:, 64:128], in_=ident[:, 0:64])

        xc = []
        xs = []
        for g in range(PASSES):
            xc.append(const.tile([P, TOK], U32, name="xc%d" % g, tag="xc%d" % g, align_bytes=64))
            xs.append(const.tile([P, TOK], U8, name="xs%d" % g, tag="xs%d" % g, align_bytes=64))

        st = {}
        spread = {}

        def bias_columns():
            bp = psum.tile([P, 512], F32, name="bp", tag="acc", bufs=2)
            nc.tensor.transpose(out=bp[:, 0:P], in_=bbf[:], identity=ident[:])
            nc.vector.tensor_copy(out=bias[:], in_=bp[:, 0:2 * HEADS])

        def tables():
            nc.scalar.activation(out=cos_t[:], in_=rc[:], func=ACT.Sin, bias=0.5 * math.pi, scale=TWO_PI)
            nc.scalar.activation(out=sin_t[:], in_=rs[:], func=ACT.Sin, scale=TWO_PI)

        def spread_transposes(half):
            for i in range(2):
                bank = psum.tile([P, 512], F32, name="tp", tag="tp", bufs=4)
                for r in range(4):
                    c = 8 * half + 4 * i + r
                    nc.tensor.transpose(out=bank[:, r * P:(r + 1) * P], in_=s_col[:, c:c + 1].to_broadcast([P, P]),
                                        identity=ident[:])
                spread[2 * half + i] = bank

        def spread_out(b, on_scalar):
            dst = scale_bc[:, b * 512:(b + 1) * 512]
            if on_scalar:
                nc.scalar.copy(out=dst, in_=spread[b][:])
            else:
                nc.vector.tensor_copy(out=dst, in_=spread[b][:])

        def widen(j, half):
            if half == 0:
                st[("wbf", j)] = work.tile([P, HID], BF16, name="wbf", tag="wbf", bufs=4)
            v_cols = HID - 512 * (j in SHARED)
            cols = slice(half * v_cols // 2, (half + 1) * v_cols // 2)
            if W_WHOLE:
                if half == 0:
                    return
                cols = slice(0, v_cols)
            nc.vector.tensor_tensor(out=st[("wbf", j)][:, cols], in0=w_in[("q", j)][:, cols].bitcast(FP8),
                                    in1=scale_bc[:, cols], op=ALU.mult)

        def cast(j):
            if j in SHARED:
                nc.scalar.copy(out=st[("wbf", j)][:, 1536:HID], in_=w_in[("q", j)][:, 1536:HID].bitcast(FP8))

        def stage_t(u):
            kind, h = units[u]
            if kind == "x":
                src = x_sb[h]
            elif kind == "k":
                src = w_in[("k", h)]
            else:
                src = st[("wbf", h)]
            words = src[:].bitcast(F32)
            if kind == "k" and h in RUNS:
                words = st[("runs", h)][:]
            if kind == "q" and h in RUNS_Q:
                words = st[("runsq", h)][:]
            banks = []
            for j in range(2):
                bank = psum.tile([P, 512], F32, name="tp", tag="tp", bufs=4)
                for gl in range(2):
                    g = 2 * j + gl
                    for e in range(2):
                        c0 = (2 * gl + e) * P
                        in_words = words[:, 256 * g + e:256 * (g + 1):2]
                        if (kind == "k" and h in RUNS) or (kind == "q" and h in RUNS_Q):
                            in_words = words[:, 256 * g + P * e:256 * g + P * (e + 1)]
                        nc.tensor.transpose(out=bank[:, c0:c0 + P], in_=in_words, identity=ident[:])
                banks.append(bank)
            st[("tp", u)] = banks

        def reorder_q(h):
            rt = work.tile([P, HID // 2], F32, name="runs", tag="runs", bufs=3)
            nc.scalar.copy(out=rt[:].rearrange("p (g e q) -> p g e q", g=PASSES, e=2),
                           in_=st[("wbf", h)][:].bitcast(F32).rearrange("p (g q e) -> p g e q", g=PASSES, e=2))
            st[("runsq", h)] = rt

        def reorder(h, half):
            if half == 0:
                st[("runs", h)] = work.tile([P, HID // 2], F32, name="runs", tag="runs", bufs=3)
            cols = slice(512 * half, 512 * (half + 1))
            nc.scalar.copy(out=st[("runs", h)][:, cols].rearrange("p (g e q) -> p g e q", g=2, e=2),
                           in_=w_in[("k", h)][:].bitcast(F32)[:, cols].rearrange("p (g q e) -> p g e q", g=2, e=2))

        def stage_e(u):
            kind, h = units[u]
            wg = work.tile([P, HID], BF16, name="wg", tag="wg", bufs=4, align_bytes=64)
            wgw = wg[:].bitcast(F32)
            for j in range(2):
                bank = st[("tp", u)][j]
                n_g = 1 if kind == "q" and j == 1 and h in SHARED else 2
                if n_g:
                    copy = nc.vector.tensor_copy if (u, j) in E_VEC else nc.scalar.copy
                    copy(out=wgw[:, 512 * j:512 * j + 256 * n_g].rearrange("p (g r e) -> p g r e", g=n_g, e=2),
                                   in_=bank[:, 0:256 * n_g].rearrange("p (g e r) -> p g r e", g=n_g, e=2))
                for gl in range(n_g, 2):
                    g = 2 * j + gl
                    for t in range(4):
                        i0 = 512 * gl + 256 * (t // 2) + t % 2
                        nc.scalar.activation(out=wg[:, 512 * g + t:512 * (g + 1):4], in_=bank[:].bitcast(BF16)[:, i0:i0 + 256 - t % 2:2],
                                             func=ACT.Copy, scale=s_t[:, 4 * g + t:4 * g + t + 1])
            st[("wg", u)] = wg

        def stage_q(u):
            kind, h = units[u]
            wg = st[("wg", u)]
            if kind == "x":
                for g in range(PASSES):
                    nc.vector.quantize_mx(out=xc[g][:, h * P:(h + 1) * P].bitcast(FP8X4),
                                          scales=xs[g][:, h * P:(h + 1) * P],
                                          in_=wg[:, g * 512:(g + 1) * 512])
            else:
                wc = work.tile([P, 512], U32, name="wc", tag="wc", bufs=4, align_bytes=64)
                ws = work.tile([P, 512], U8, name="ws", tag="ws", bufs=4, align_bytes=64)
                nc.vector.quantize_mx(out=wc[:].bitcast(FP8X4), scales=ws[:], in_=wg[:])
                st[("wc", u)] = (wc, ws)

        def token_parts(u):
            n = 2 if u == n_units - 1 else 1
            return [slice(i * TOK // n, (i + 1) * TOK // n) for i in range(n)]

        def stage_m(u):
            wc, ws = st[("wc", u)]
            for cols in token_parts(u):
                acc = psum.tile([P, 512], F32, name="acc", tag="acc", bufs=2)
                for g in range(PASSES):
                    nc.tensor.matmul_mx(out=acc[:, cols], lhsT=wc[:, g * P:(g + 1) * P].bitcast(FP8X4),
                                        lhsT_scale=ws[:, g * P:(g + 1) * P],
                                        rhs=xc[g][:, cols].bitcast(FP8X4), rhs_scale=xs[g][:, cols],
                                        start=(g == 0), stop=(g == PASSES - 1))
                st[("acc", u, cols.start)] = acc

        def stage_z(u):
            kind, h = units[u]
            col = h if kind == "q" else HEADS + h
            z1 = work.tile([P, TOK], F32, name="z1", tag="z1", bufs=4)
            z2 = work.tile([P, TOK], F32, name="z2", tag="z2", bufs=4)
            for cols in token_parts(u):
                acc = st[("acc", u, cols.start)]
                for z, table in ((z1, cos_t), (z2, sin_t)):
                    nc.vector.scalar_tensor_tensor(out=z[:, cols], in0=acc[:, cols], scalar=bias[:, col:col + 1],
                                                   in1=table[:, cols], op0=ALU.add, op1=ALU.mult)
            st[("z", u)] = (z1, z2)

        def stage_f(u):
            z1, z2 = st[("z", u)]
            for part in token_parts(u):
                if u == n_units - 1:
                    fin = psum.tile([P, 512], F32, name="fin", tag="tp", bufs=4)
                else:
                    fin = psum.tile([P, 512], F32, name="fin", tag="fin", bufs=2)
                for c0 in range(part.start, part.stop, P):
                    cols = slice(c0, c0 + P)
                    nc.tensor.matmul(out=fin[:, cols], lhsT=z1[:, cols], rhs=ident[:], is_transpose=True,
                                     start=True, stop=False)
                    nc.tensor.matmul(out=fin[:, cols], lhsT=z2[:, cols], rhs=perm[:], is_transpose=True,
                                     start=False, stop=True)
                st[("fin", u, part.start)] = fin

        def stage_o(u):
            kind, h = units[u]
            dst = out_0 if kind == "q" else out_1
            ob = work.tile([P, TOK], F32, name="ob", tag="ob", bufs=6)
            for part in token_parts(u):
                nc.scalar.copy(out=ob[:, part], in_=st[("fin", u, part.start)][:, part])
                queue = nc.sync if part.start == 0 else nc.scalar
                queue.dma_start(out=dst[0, h].rearrange("(p a) d -> p (a d)", a=4)[:, part], in_=ob[:, part])

        widen_at = {}
        step = n_units
        for h in reversed(range(HEADS)):
            for half in (1, 0):
                step = min(step - 1, units.index(("q", h)) - 2)
                widen_at.setdefault(max(step, W_FIRST + (2 * h + half) // 2), []).append((h, half))

        def is_head(u):
            return n_x <= u < n_units

        q_at, m_at, z_at, f_at = {}, {}, {}, {}
        for u in range(n_units):
            q_at[u] = u + 1 if u < n_x + RAMP else min(u + LQ, n_units + QE)
            if u >= n_x:
                m_at[u] = max(q_at[u] + 1, m_at.get(u - 1, 0) + (1 if u < n_units - 1 else 1))
                z_at[u] = m_at[u] + 1
                f_at[u] = z_at[u] + 1

        def due(at, s):
            return [u for u in sorted(at) if at[u] == s]

        for u in range(f_at[n_units - 1] + 1):
            if u < n_units:
                stage_t(u)
                stage_e(u)
            for half in (0, 1):
                ro = u + RO_LEAD - half
                if ro < n_units and units[ro][0] == "k" and units[ro][1] in RUNS:
                    reorder(units[ro][1], half)
            if u == T_BIAS:
                bias_columns()
            if u == T_TABLES:
                tables()
            for half in (0, 1):
                if u == SP[half]:
                    spread_transposes(half)
            q_last = u >= PAIR_FROM and u % 2 == PAR and u < n_units
            if not q_last:
                for v in due(q_at, u):
                    stage_q(v)
            for half in (0, 1):
                if u == SP[half]:
                    for b in (2 * half, 2 * half + 1):
                        spread_out(b, b in EV_SCALAR)
            if u >= n_units:
                for v in due(m_at, u):
                    stage_m(v)
            for v in due(f_at, u):
                stage_f(v)
                stage_o(v)
            if u < n_units:
                for v in due(m_at, u):
                    stage_m(v)
            for v in due(z_at, u):
                stage_z(v)
            for j, half in reversed(widen_at.get(u, [])):
                widen(j, half)
                if half == 0:
                    cast(j)
            if q_last:
                for v in due(q_at, u):
                    stage_q(v)
